import numpy as np
import ml_dtypes


def mxq(x, axis, fmt="e4m3"):
    dtype, down = {"e4m3": (ml_dtypes.float8_e4m3fn, 7), "e5m2": (ml_dtypes.float8_e5m2, 14)}[fmt]
    v = np.moveaxis(np.asarray(x, np.float32).astype(ml_dtypes.bfloat16).astype(np.float64), axis, -1)
    blocks = v.reshape(v.shape[:-1] + (-1, 32))
    amax = np.abs(blocks).max(-1, keepdims=True)
    byte = np.maximum(np.where(amax > 0, np.frexp(amax)[1] - 1 + 127, 0) - down, 1)
    scale = np.exp2(byte - 127.0)
    codes = (blocks / scale).astype(np.float32).astype(dtype).astype(np.float64)
    return np.moveaxis((codes * scale).reshape(v.shape), -1, axis)


WIDE = False


def mx_kscale(k):
    if not WIDE:
        return np.ones(k)
    levels = np.array([10, -10, 5, -5, 0])
    a = np.random.permutation(np.resize(levels, k // 512 * 4)).reshape(k // 512, 4)
    idx = np.arange(k)
    return np.exp2(a[idx // 512, idx % 128 // 32])


BF16 = ml_dtypes.bfloat16


def bf(x):
    return np.asarray(x, np.float32).astype(BF16)


def f64(x):
    return np.asarray(x).astype(np.float64)


ND, NS, D0, D1, D2, D3, DH, C = 2048, 2048, 512, 128, 256, 512, 256, 10
SIG = 4.0


def draw_adj():
    w = np.exp(SIG * np.random.standard_normal((ND, NS)))
    return w / w.sum(1, keepdims=True)


def setup_inputs():
    s = mx_kscale(D0)
    return {"x": bf(np.random.standard_normal((NS, D0)) * s),
            "adj": bf(draw_adj()),
            "W0": bf(np.random.standard_normal((D0, D1)) * 2.0 / np.sqrt(D0) / s[:, None]),
            "b0": bf(np.random.standard_normal(D1) * 0.5)}


def reference(x, adj, W0, b0):
    h = (mxq(f64(x), 1, "e4m3") @ mxq(f64(W0), 0, "e4m3")) + f64(b0)
    return np.maximum(mxq(f64(adj), 1, "e4m3") @ mxq(h, 0, "e4m3"), 0.0)

@@ -1,0 +1,183 @@
+from contextlib import ExitStack
+
+import concourse.mybir as mybir
+from concourse.masks import make_identity
+
+F32 = mybir.dt.float32
+BF16 = mybir.dt.bfloat16
+U32 = mybir.dt.uint32
+U8 = mybir.dt.uint8
+FP8X4 = mybir.dt.float8_e4m3fn_x4
+
+P = 128
+PACK = 4
+K_PASS = P * PACK
+BANK_WORDS = 512
+
+NODES = 2048
+FEATS = 512
+HID = 128
+PASSES = NODES // K_PASS
+CHUNK_TILES = 2
+CHUNKS = NODES // (CHUNK_TILES * P)
+CHUNK_BANKS = CHUNK_TILES * NODES // (2 * BANK_WORDS)
+VECTOR_BANK = 2
+
+FLOPS = 2 * NODES * FEATS * HID + 2 * NODES * NODES * HID
+
+
+def tile_gcn_pa_kernel(tc, x, adj, W0, b0, out):
+    nc = tc.nc
+    with ExitStack() as ctx:
+        keep = ctx.enter_context(tc.tile_pool(name="keep", bufs=1))
+        grouped_pool = ctx.enter_context(tc.tile_pool(name="grouped", bufs=3))
+        codes_pool = ctx.enter_context(tc.tile_pool(name="codes", bufs=4))
+        result_pool = ctx.enter_context(tc.tile_pool(name="result", bufs=4))
+        flip_pool = ctx.enter_context(tc.psum_pool(name="flip", bufs=6))
+        acc_pool = ctx.enter_context(tc.psum_pool(name="acc", bufs=2))
+        ctx.enter_context(tc.manual_schedule())
+
+        w_rows = keep.tile([P, PACK, HID], BF16, name="w_rows")
+        nc.scalar.dma_start(
+            out=w_rows[:].rearrange("p (u e) c -> p u (e c)", u=2),
+            in_=W0.rearrange("(u p e) c -> p u (e c)", u=2, e=2),
+        )
+        bias = keep.tile([P, HID], BF16, name="bias")
+        nc.scalar.dma_start(out=bias[:], in_=b0.partition_broadcast(P))
+
+        x_view = x.rearrange("(c p e) f -> p c (e f)", p=P, e=2)
+        x_rows = []
+        for g in range(PASSES):
+            x_piece = keep.tile([P, PACK * FEATS], BF16, name="x_rows%d" % g)
+            nc.sync.dma_start(
+                out=x_piece[:].rearrange("p (c w) -> p c w", c=2),
+                in_=x_view[:, 2 * g : 2 * g + 2, :],
+            )
+            x_rows.append(x_piece)
+
+        adj_view = adj.rearrange("(b p c) j -> b p (c j)", p=P, c=CHUNK_TILES)
+        out_view = out.rearrange("(b p c) d -> b p (c d)", p=P, c=CHUNK_TILES)
+        adj_rows = []
+        for b in range(CHUNKS):
+            adj_piece = keep.tile([P, CHUNK_TILES * NODES], BF16, name="adj_rows%d" % b)
+            nc.sync.dma_start(out=adj_piece[:], in_=adj_view[b])
+            adj_rows.append(adj_piece)
+
+        ident = keep.tile([P, P], F32, name="ident")
+        make_identity(nc, ident[:])
+
+        w_grouped = keep.tile([P, HID, PACK], BF16, name="w_grouped", align_bytes=64)
+        nc.vector.tensor_copy(out=w_grouped[:], in_=w_rows[:].rearrange("p t c -> p c t"))
+        w_codes = keep.tile([P, HID], U32, name="w_codes", align_bytes=64)
+        w_scales = keep.tile([P, HID], U8, name="w_scales", align_bytes=64)
+        nc.vector.quantize_mx(
+            out=w_codes[:].bitcast(FP8X4),
+            scales=w_scales[:],
+            in_=w_grouped[:].rearrange("p c t -> p (c t)"),
+        )
+
+        def flip_words(src_words, dst_words, copy):
+            bank = flip_pool.tile([P, BANK_WORDS], F32, name="bank")
+            for q in range(BANK_WORDS // P):
+                cols = slice(q * P, (q + 1) * P)
+                nc.tensor.transpose(bank[:, cols], src_words[:, cols], ident[:])
+            copy(
+                out=dst_words.rearrange("p (a r u) -> p a r u", a=2, u=2),
+                in_=bank[:].rearrange("p (a u r) -> p a r u", a=2, u=2),
+            )
+
+        x_codes = keep.tile([P, PASSES * K_PASS], U32, name="x_codes", align_bytes=64)
+        x_scales = keep.tile([P, PASSES * K_PASS], U8, name="x_scales", align_bytes=64)
+        h_grouped = keep.tile([P, PASSES * HID * PACK], BF16, name="h_grouped", align_bytes=64)
+
+        def quantise_x(g):
+            src_words = x_rows[g][:].bitcast(F32)
+            x_grouped = keep.tile([P, PACK * FEATS], BF16, name="x_grouped%d" % g, align_bytes=64)
+            dst_words = x_grouped[:].bitcast(F32)
+            for k in range(2):
+                words = slice(k * BANK_WORDS, (k + 1) * BANK_WORDS)
+                flip_words(src_words[:, words], dst_words[:, words], nc.scalar.copy)
+            cols = slice(g * K_PASS, (g + 1) * K_PASS)
+            nc.vector.quantize_mx(
+                out=x_codes[:, cols].bitcast(FP8X4), scales=x_scales[:, cols], in_=x_grouped[:]
+            )
+
+        def hidden(g):
+            h_sum = acc_pool.tile([P, PACK * HID], F32, name="h_sum", tag="acc")
+            for t in range(PACK):
+                rows = slice((PACK * g + t) * P, (PACK * g + t + 1) * P)
+                nc.tensor.matmul_mx(
+                    out=h_sum[:, t * HID : (t + 1) * HID],
+                    lhsT=x_codes[:, rows].bitcast(FP8X4),
+                    lhsT_scale=x_scales[:, rows],
+                    rhs=w_codes[:].bitcast(FP8X4),
+                    rhs_scale=w_scales[:],
+                    start=True,
+                    stop=True,
+                )
+            cols = slice(g * HID * PACK, (g + 1) * HID * PACK)
+            nc.vector.tensor_tensor(
+                out=h_grouped[:, cols].rearrange("p (d t) -> p d t", t=PACK),
+                in0=h_sum[:].rearrange("p (t d) -> p d t", t=PACK),
+                in1=bias[:].unsqueeze(2).to_broadcast([P, HID, PACK]),
+                op=mybir.AluOpType.add,
+            )
+
+        quantise_x(0)
+        for g in range(1, PASSES):
+            quantise_x(g)
+            hidden(g - 1)
+        hidden(PASSES - 1)
+
+        h_codes = keep.tile([P, PASSES * HID], U32, name="h_codes", align_bytes=64)
+        h_scales = keep.tile([P, PASSES * HID], U8, name="h_scales", align_bytes=64)
+        nc.vector.quantize_mx(out=h_codes[:].bitcast(FP8X4), scales=h_scales[:], in_=h_grouped[:])
+
+        def quantise_adj(b):
+            src_words = adj_rows[b][:].bitcast(F32)
+            adj_grouped = grouped_pool.tile(
+                [P, CHUNK_TILES * NODES], BF16, name="adj_grouped", align_bytes=64
+            )
+            dst_words = adj_grouped[:].bitcast(F32)
+            for k in range(CHUNK_BANKS):
+                words = slice(k * BANK_WORDS, (k + 1) * BANK_WORDS)
+                copy = nc.vector.tensor_copy if k == VECTOR_BANK else nc.scalar.copy
+                flip_words(src_words[:, words], dst_words[:, words], copy)
+            adj_codes = codes_pool.tile(
+                [P, CHUNK_TILES * PASSES * P], U32, name="adj_codes", align_bytes=64
+            )
+            adj_scales = codes_pool.tile(
+                [P, CHUNK_TILES * PASSES * P], U8, name="adj_scales", align_bytes=64
+            )
+            for c in range(CHUNK_TILES):
+                nc.vector.quantize_mx(
+                    out=adj_codes[:, c * PASSES * P : (c + 1) * PASSES * P].bitcast(FP8X4),
+                    scales=adj_scales[:, c * PASSES * P : (c + 1) * PASSES * P],
+                    in_=adj_grouped[:, c * NODES : (c + 1) * NODES],
+                )
+            return adj_codes, adj_scales
+
+        def aggregate(b, adj_codes, adj_scales):
+            out_sum = acc_pool.tile([P, CHUNK_TILES * HID], F32, name="out_sum", tag="acc")
+            for c in range(CHUNK_TILES):
+                for g in range(PASSES):
+                    rows = slice((c * PASSES + g) * P, (c * PASSES + g + 1) * P)
+                    nc.tensor.matmul_mx(
+                        out=out_sum[:, c * HID : (c + 1) * HID],
+                        lhsT=adj_codes[:, rows].bitcast(FP8X4),
+                        lhsT_scale=adj_scales[:, rows],
+                        rhs=h_codes[:, g * HID : (g + 1) * HID].bitcast(FP8X4),
+                        rhs_scale=h_scales[:, g * HID : (g + 1) * HID],
+                        start=(g == 0),
+                        stop=(g == PASSES - 1),
+                    )
+            result = result_pool.tile([P, CHUNK_TILES * HID], F32, name="result")
+            nc.vector.tensor_scalar_max(out=result[:], in0=out_sum[:], scalar1=0.0)
+            nc.sync.dma_start(out=out_view[b], in_=result[:])
+
+        quantised = quantise_adj(0)
+        for b in range(1, CHUNKS):
+            following = quantise_adj(b)
+            aggregate(b - 1, quantised[0], quantised[1])
+            quantised = following
+        aggregate(CHUNKS - 1, quantised[0], quantised[1])

@@ -22,6 +22,7 @@ CHUNK_TILES = 2
 CHUNKS = NODES // (CHUNK_TILES * P)
 CHUNK_BANKS = CHUNK_TILES * NODES // (2 * BANK_WORDS)
 VECTOR_BANK = 2
+LAG = 2
 
 FLOPS = 2 * NODES * FEATS * HID + 2 * NODES * NODES * HID
 
@@ -37,13 +38,14 @@ def tile_gcn_pa_kernel(tc, x, adj, W0, b0, out):
         acc_pool = ctx.enter_context(tc.psum_pool(name="acc", bufs=2))
         ctx.enter_context(tc.manual_schedule())
 
+        b_row = keep.tile([1, HID], BF16, name="b_row")
+        nc.sync.dma_start(out=b_row[:], in_=b0.rearrange("(o d) -> o d", o=1))
+
         w_rows = keep.tile([P, PACK, HID], BF16, name="w_rows")
         nc.scalar.dma_start(
             out=w_rows[:].rearrange("p (u e) c -> p u (e c)", u=2),
             in_=W0.rearrange("(u p e) c -> p u (e c)", u=2, e=2),
         )
-        bias = keep.tile([P, HID], BF16, name="bias")
-        nc.scalar.dma_start(out=bias[:], in_=b0.partition_broadcast(P))
 
         x_view = x.rearrange("(c p e) f -> p c (e f)", p=P, e=2)
         x_rows = []
@@ -66,6 +68,16 @@ def tile_gcn_pa_kernel(tc, x, adj, W0, b0, out):
         ident = keep.tile([P, P], F32, name="ident")
         make_identity(nc, ident[:])
 
+        ones = keep.tile([P, P], BF16, name="ones")
+        nc.vector.memset(ones[:], 1.0)
+        b_rows = keep.tile([P, HID], BF16, name="b_rows")
+        nc.vector.memset(b_rows[:], 0.0)
+        nc.vector.tensor_copy(out=b_rows[0:1, :], in_=b_row[:])
+        bias_sum = acc_pool.tile([P, HID], F32, name="bias_sum", tag="acc")
+        nc.tensor.matmul(out=bias_sum[:], lhsT=ones[:], rhs=b_rows[:], start=True, stop=True)
+        bias = keep.tile([P, HID], F32, name="bias")
+        nc.scalar.activation(out=bias[:], in_=bias_sum[:], func=mybir.ActivationFunctionType.Copy)
+
         w_grouped = keep.tile([P, HID, PACK], BF16, name="w_grouped", align_bytes=64)
         nc.vector.tensor_copy(out=w_grouped[:], in_=w_rows[:].rearrange("p t c -> p c t"))
         w_codes = keep.tile([P, HID], U32, name="w_codes", align_bytes=64)
@@ -86,23 +98,29 @@ def tile_gcn_pa_kernel(tc, x, adj, W0, b0, out):
                 in_=bank[:].rearrange("p (a u r) -> p a r u", a=2, u=2),
             )
 
+        x_grouped = []
         x_codes = keep.tile([P, PASSES * K_PASS], U32, name="x_codes", align_bytes=64)
         x_scales = keep.tile([P, PASSES * K_PASS], U8, name="x_scales", align_bytes=64)
         h_grouped = keep.tile([P, PASSES * HID * PACK], BF16, name="h_grouped", align_bytes=64)
+        h_codes = keep.tile([P, PASSES * HID], U32, name="h_codes", align_bytes=64)
+        h_scales = keep.tile([P, PASSES * HID], U8, name="h_scales", align_bytes=64)
 
-        def quantise_x(g):
+        def flip_x(g):
+            grouped = keep.tile([P, PACK * FEATS], BF16, name="x_grouped%d" % g, align_bytes=64)
             src_words = x_rows[g][:].bitcast(F32)
-            x_grouped = keep.tile([P, PACK * FEATS], BF16, name="x_grouped%d" % g, align_bytes=64)
-            dst_words = x_grouped[:].bitcast(F32)
-            for k in range(2):
+            dst_words = grouped[:].bitcast(F32)
+            for k in range(PACK * FEATS // (2 * BANK_WORDS)):
                 words = slice(k * BANK_WORDS, (k + 1) * BANK_WORDS)
                 flip_words(src_words[:, words], dst_words[:, words], nc.scalar.copy)
+            x_grouped.append(grouped)
+
+        def quantise_x(g):
             cols = slice(g * K_PASS, (g + 1) * K_PASS)
             nc.vector.quantize_mx(
-                out=x_codes[:, cols].bitcast(FP8X4), scales=x_scales[:, cols], in_=x_grouped[:]
+                out=x_codes[:, cols].bitcast(FP8X4), scales=x_scales[:, cols], in_=x_grouped[g][:]
             )
 
-        def hidden(g):
+        def multiply_x(g):
             h_sum = acc_pool.tile([P, PACK * HID], F32, name="h_sum", tag="acc")
             for t in range(PACK):
                 rows = slice((PACK * g + t) * P, (PACK * g + t + 1) * P)
@@ -122,62 +140,76 @@ def tile_gcn_pa_kernel(tc, x, adj, W0, b0, out):
                 in1=bias[:].unsqueeze(2).to_broadcast([P, HID, PACK]),
                 op=mybir.AluOpType.add,
             )
+            nc.vector.quantize_mx(
+                out=h_codes[:, g * HID : (g + 1) * HID].bitcast(FP8X4),
+                scales=h_scales[:, g * HID : (g + 1) * HID],
+                in_=h_grouped[:, cols],
+            )
 
-        quantise_x(0)
-        for g in range(1, PASSES):
-            quantise_x(g)
-            hidden(g - 1)
-        hidden(PASSES - 1)
+        adj_grouped = []
+        adj_codes = []
+        adj_scales = []
 
-        h_codes = keep.tile([P, PASSES * HID], U32, name="h_codes", align_bytes=64)
-        h_scales = keep.tile([P, PASSES * HID], U8, name="h_scales", align_bytes=64)
-        nc.vector.quantize_mx(out=h_codes[:].bitcast(FP8X4), scales=h_scales[:], in_=h_grouped[:])
-
-        def quantise_adj(b):
-            src_words = adj_rows[b][:].bitcast(F32)
-            adj_grouped = grouped_pool.tile(
+        def flip_adj(b):
+            grouped = grouped_pool.tile(
                 [P, CHUNK_TILES * NODES], BF16, name="adj_grouped", align_bytes=64
             )
-            dst_words = adj_grouped[:].bitcast(F32)
+            src_words = adj_rows[b][:].bitcast(F32)
+            dst_words = grouped[:].bitcast(F32)
             for k in range(CHUNK_BANKS):
                 words = slice(k * BANK_WORDS, (k + 1) * BANK_WORDS)
                 copy = nc.vector.tensor_copy if k == VECTOR_BANK else nc.scalar.copy
                 flip_words(src_words[:, words], dst_words[:, words], copy)
-            adj_codes = codes_pool.tile(
+            adj_grouped.append(grouped)
+
+        def quantise_adj(b):
+            codes = codes_pool.tile(
                 [P, CHUNK_TILES * PASSES * P], U32, name="adj_codes", align_bytes=64
             )
-            adj_scales = codes_pool.tile(
+            scales = codes_pool.tile(
                 [P, CHUNK_TILES * PASSES * P], U8, name="adj_scales", align_bytes=64
             )
             for c in range(CHUNK_TILES):
                 nc.vector.quantize_mx(
-                    out=adj_codes[:, c * PASSES * P : (c + 1) * PASSES * P].bitcast(FP8X4),
-                    scales=adj_scales[:, c * PASSES * P : (c + 1) * PASSES * P],
-                    in_=adj_grouped[:, c * NODES : (c + 1) * NODES],
+                    out=codes[:, c * PASSES * P : (c + 1) * PASSES * P].bitcast(FP8X4),
+                    scales=scales[:, c * PASSES * P : (c + 1) * PASSES * P],
+                    in_=adj_grouped[b][:, c * NODES : (c + 1) * NODES],
                 )
-            return adj_codes, adj_scales
+            adj_codes.append(codes)
+            adj_scales.append(scales)
 
-        def aggregate(b, adj_codes, adj_scales):
+        def multiply_adj(b):
             out_sum = acc_pool.tile([P, CHUNK_TILES * HID], F32, name="out_sum", tag="acc")
             for c in range(CHUNK_TILES):
                 for g in range(PASSES):
                     rows = slice((c * PASSES + g) * P, (c * PASSES + g + 1) * P)
                     nc.tensor.matmul_mx(
                         out=out_sum[:, c * HID : (c + 1) * HID],
-                        lhsT=adj_codes[:, rows].bitcast(FP8X4),
-                        lhsT_scale=adj_scales[:, rows],
+                        lhsT=adj_codes[b][:, rows].bitcast(FP8X4),
+                        lhsT_scale=adj_scales[b][:, rows],
                         rhs=h_codes[:, g * HID : (g + 1) * HID].bitcast(FP8X4),
                         rhs_scale=h_scales[:, g * HID : (g + 1) * HID],
                         start=(g == 0),
                         stop=(g == PASSES - 1),
                     )
             result = result_pool.tile([P, CHUNK_TILES * HID], F32, name="result")
-            nc.vector.tensor_scalar_max(out=result[:], in0=out_sum[:], scalar1=0.0)
+            nc.scalar.activation(
+                out=result[:], in_=out_sum[:], func=mybir.ActivationFunctionType.Relu
+            )
             nc.sync.dma_start(out=out_view[b], in_=result[:])
 
-        quantised = quantise_adj(0)
-        for b in range(1, CHUNKS):
-            following = quantise_adj(b)
-            aggregate(b - 1, quantised[0], quantised[1])
-            quantised = following
-        aggregate(CHUNKS - 1, quantised[0], quantised[1])
+        steps = PASSES + CHUNKS
+        for step in range(steps + LAG):
+            if step < PASSES:
+                flip_x(step)
+            elif step < steps:
+                flip_adj(step - PASSES)
+            ready = step - LAG
+            if 0 <= ready < PASSES:
+                multiply_x(ready)
+            elif ready >= PASSES:
+                multiply_adj(ready - PASSES)
+            if step < PASSES:
+                quantise_x(step)
+            elif step < steps:
+                quantise_adj(step - PASSES)

@@ -23,6 +23,7 @@ CHUNKS = NODES // (CHUNK_TILES * P)
 CHUNK_BANKS = CHUNK_TILES * NODES // (2 * BANK_WORDS)
 VECTOR_BANK = 2
 LAG = 2
+FILL_STEPS = PASSES + LAG
 
 FLOPS = 2 * NODES * FEATS * HID + 2 * NODES * NODES * HID
 
@@ -34,7 +35,8 @@ def tile_gcn_pa_kernel(tc, x, adj, W0, b0, out):
         grouped_pool = ctx.enter_context(tc.tile_pool(name="grouped", bufs=3))
         codes_pool = ctx.enter_context(tc.tile_pool(name="codes", bufs=4))
         result_pool = ctx.enter_context(tc.tile_pool(name="result", bufs=4))
-        flip_pool = ctx.enter_context(tc.psum_pool(name="flip", bufs=6))
+        flip_pool = ctx.enter_context(tc.psum_pool(name="flip", bufs=5))
+        idle_pool = ctx.enter_context(tc.psum_pool(name="idle", bufs=1))
         acc_pool = ctx.enter_context(tc.psum_pool(name="acc", bufs=2))
         ctx.enter_context(tc.manual_schedule())
 
@@ -77,6 +79,13 @@ def tile_gcn_pa_kernel(tc, x, adj, W0, b0, out):
         nc.tensor.matmul(out=bias_sum[:], lhsT=ones[:], rhs=b_rows[:], start=True, stop=True)
         bias = keep.tile([P, HID], F32, name="bias")
         nc.scalar.activation(out=bias[:], in_=bias_sum[:], func=mybir.ActivationFunctionType.Copy)
+
+        zeros = keep.tile([P, BANK_WORDS], BF16, name="zeros")
+        nc.vector.memset(zeros[:], 0.0)
+        idle_sum = idle_pool.tile([P, BANK_WORDS], F32, name="idle_sum")
+
+        def keep_clock_up():
+            nc.tensor.matmul(out=idle_sum[:], lhsT=ones[:], rhs=zeros[:], start=True, stop=True)
 
         w_grouped = keep.tile([P, HID, PACK], BF16, name="w_grouped", align_bytes=64)
         nc.vector.tensor_copy(out=w_grouped[:], in_=w_rows[:].rearrange("p t c -> p c t"))
@@ -204,6 +213,8 @@ def tile_gcn_pa_kernel(tc, x, adj, W0, b0, out):
                 flip_x(step)
             elif step < steps:
                 flip_adj(step - PASSES)
+            if step < FILL_STEPS:
+                keep_clock_up()
             ready = step - LAG
             if 0 <= ready < PASSES:
                 multiply_x(ready)

@@ -23,7 +23,7 @@ CHUNKS = NODES // (CHUNK_TILES * P)
 CHUNK_BANKS = CHUNK_TILES * NODES // (2 * BANK_WORDS)
 VECTOR_BANK = 2
 LAG = 2
-FILL_STEPS = PASSES + LAG
+WARM_UPS = 6
 
 FLOPS = 2 * NODES * FEATS * HID + 2 * NODES * NODES * HID
 
@@ -72,20 +72,23 @@ def tile_gcn_pa_kernel(tc, x, adj, W0, b0, out):
 
         ones = keep.tile([P, P], BF16, name="ones")
         nc.vector.memset(ones[:], 1.0)
-        b_rows = keep.tile([P, HID], BF16, name="b_rows")
-        nc.vector.memset(b_rows[:], 0.0)
-        nc.vector.tensor_copy(out=b_rows[0:1, :], in_=b_row[:])
-        bias_sum = acc_pool.tile([P, HID], F32, name="bias_sum", tag="acc")
-        nc.tensor.matmul(out=bias_sum[:], lhsT=ones[:], rhs=b_rows[:], start=True, stop=True)
-        bias = keep.tile([P, HID], F32, name="bias")
-        nc.scalar.activation(out=bias[:], in_=bias_sum[:], func=mybir.ActivationFunctionType.Copy)
-
         zeros = keep.tile([P, BANK_WORDS], BF16, name="zeros")
         nc.vector.memset(zeros[:], 0.0)
+        b_rows = keep.tile([P, HID], BF16, name="b_rows")
+        nc.vector.memset(b_rows[:], 0.0)
         idle_sum = idle_pool.tile([P, BANK_WORDS], F32, name="idle_sum")
-
-        def keep_clock_up():
+        for warm_up in range(WARM_UPS):
             nc.tensor.matmul(out=idle_sum[:], lhsT=ones[:], rhs=zeros[:], start=True, stop=True)
+
+        bias = keep.tile([P, HID], F32, name="bias")
+
+        def spread_bias():
+            nc.vector.tensor_copy(out=b_rows[0:1, :], in_=b_row[:])
+            bias_sum = acc_pool.tile([P, HID], F32, name="bias_sum", tag="acc")
+            nc.tensor.matmul(out=bias_sum[:], lhsT=ones[:], rhs=b_rows[:], start=True, stop=True)
+            nc.scalar.activation(
+                out=bias[:], in_=bias_sum[:], func=mybir.ActivationFunctionType.Copy
+            )
 
         w_grouped = keep.tile([P, HID, PACK], BF16, name="w_grouped", align_bytes=64)
         nc.vector.tensor_copy(out=w_grouped[:], in_=w_rows[:].rearrange("p t c -> p c t"))
@@ -213,8 +216,8 @@ def tile_gcn_pa_kernel(tc, x, adj, W0, b0, out):
                 flip_x(step)
             elif step < steps:
                 flip_adj(step - PASSES)
-            if step < FILL_STEPS:
-                keep_clock_up()
+            if step == 0:
+                spread_bias()
             ready = step - LAG
             if 0 <= ready < PASSES:
                 multiply_x(ready)

@@ -21,8 +21,8 @@ PASSES = NODES // K_PASS
 CHUNK_TILES = 2
 CHUNKS = NODES // (CHUNK_TILES * P)
 CHUNK_BANKS = CHUNK_TILES * NODES // (2 * BANK_WORDS)
-VECTOR_BANK = 2
-LAG = 2
+VECTOR_BANK = 3
+LAST_VECTOR_BANK = 1
 WARM_UPS = 6
 
 FLOPS = 2 * NODES * FEATS * HID + 2 * NODES * NODES * HID
@@ -32,11 +32,10 @@ def tile_gcn_pa_kernel(tc, x, adj, W0, b0, out):
     nc = tc.nc
     with ExitStack() as ctx:
         keep = ctx.enter_context(tc.tile_pool(name="keep", bufs=1))
-        grouped_pool = ctx.enter_context(tc.tile_pool(name="grouped", bufs=3))
-        codes_pool = ctx.enter_context(tc.tile_pool(name="codes", bufs=4))
+        grouped_pool = ctx.enter_context(tc.tile_pool(name="grouped", bufs=4))
+        codes_pool = ctx.enter_context(tc.tile_pool(name="codes", bufs=6))
         result_pool = ctx.enter_context(tc.tile_pool(name="result", bufs=4))
-        flip_pool = ctx.enter_context(tc.psum_pool(name="flip", bufs=5))
-        idle_pool = ctx.enter_context(tc.psum_pool(name="idle", bufs=1))
+        flip_pool = ctx.enter_context(tc.psum_pool(name="flip", bufs=6))
         acc_pool = ctx.enter_context(tc.psum_pool(name="acc", bufs=2))
         ctx.enter_context(tc.manual_schedule())
 
@@ -64,7 +63,11 @@ def tile_gcn_pa_kernel(tc, x, adj, W0, b0, out):
         adj_rows = []
         for b in range(CHUNKS):
             adj_piece = keep.tile([P, CHUNK_TILES * NODES], BF16, name="adj_rows%d" % b)
-            nc.sync.dma_start(out=adj_piece[:], in_=adj_view[b])
+            parts = 2 if b == CHUNKS - 1 else 1
+            for part in range(parts):
+                width = CHUNK_TILES * NODES // parts
+                cols = slice(part * width, (part + 1) * width)
+                nc.sync.dma_start(out=adj_piece[:, cols], in_=adj_view[b][:, cols])
             adj_rows.append(adj_piece)
 
         ident = keep.tile([P, P], F32, name="ident")
@@ -76,7 +79,7 @@ def tile_gcn_pa_kernel(tc, x, adj, W0, b0, out):
         nc.vector.memset(zeros[:], 0.0)
         b_rows = keep.tile([P, HID], BF16, name="b_rows")
         nc.vector.memset(b_rows[:], 0.0)
-        idle_sum = idle_pool.tile([P, BANK_WORDS], F32, name="idle_sum")
+        idle_sum = flip_pool.tile([P, BANK_WORDS], F32, name="idle_sum", tag="bank")
         for warm_up in range(WARM_UPS):
             nc.tensor.matmul(out=idle_sum[:], lhsT=ones[:], rhs=zeros[:], start=True, stop=True)
 
@@ -101,7 +104,7 @@ def tile_gcn_pa_kernel(tc, x, adj, W0, b0, out):
         )
 
         def flip_words(src_words, dst_words, copy):
-            bank = flip_pool.tile([P, BANK_WORDS], F32, name="bank")
+            bank = flip_pool.tile([P, BANK_WORDS], F32, name="bank", tag="bank")
             for q in range(BANK_WORDS // P):
                 cols = slice(q * P, (q + 1) * P)
                 nc.tensor.transpose(bank[:, cols], src_words[:, cols], ident[:])
@@ -111,6 +114,7 @@ def tile_gcn_pa_kernel(tc, x, adj, W0, b0, out):
             )
 
         x_grouped = []
+        h_sums = []
         x_codes = keep.tile([P, PASSES * K_PASS], U32, name="x_codes", align_bytes=64)
         x_scales = keep.tile([P, PASSES * K_PASS], U8, name="x_scales", align_bytes=64)
         h_grouped = keep.tile([P, PASSES * HID * PACK], BF16, name="h_grouped", align_bytes=64)
@@ -145,13 +149,19 @@ def tile_gcn_pa_kernel(tc, x, adj, W0, b0, out):
                     start=True,
                     stop=True,
                 )
+            h_sums.append(h_sum)
+
+        def add_bias(g):
             cols = slice(g * HID * PACK, (g + 1) * HID * PACK)
             nc.vector.tensor_tensor(
                 out=h_grouped[:, cols].rearrange("p (d t) -> p d t", t=PACK),
-                in0=h_sum[:].rearrange("p (t d) -> p d t", t=PACK),
+                in0=h_sums[g][:].rearrange("p (t d) -> p d t", t=PACK),
                 in1=bias[:].unsqueeze(2).to_broadcast([P, HID, PACK]),
                 op=mybir.AluOpType.add,
             )
+
+        def quantise_h(g):
+            cols = slice(g * HID * PACK, (g + 1) * HID * PACK)
             nc.vector.quantize_mx(
                 out=h_codes[:, g * HID : (g + 1) * HID].bitcast(FP8X4),
                 scales=h_scales[:, g * HID : (g + 1) * HID],
@@ -170,60 +180,112 @@ def tile_gcn_pa_kernel(tc, x, adj, W0, b0, out):
             dst_words = grouped[:].bitcast(F32)
             for k in range(CHUNK_BANKS):
                 words = slice(k * BANK_WORDS, (k + 1) * BANK_WORDS)
-                copy = nc.vector.tensor_copy if k == VECTOR_BANK else nc.scalar.copy
+                mine = LAST_VECTOR_BANK if b == CHUNKS - 1 else VECTOR_BANK
+                copy = nc.vector.tensor_copy if k == mine else nc.scalar.copy
                 flip_words(src_words[:, words], dst_words[:, words], copy)
             adj_grouped.append(grouped)
 
-        def quantise_adj(b):
-            codes = codes_pool.tile(
-                [P, CHUNK_TILES * PASSES * P], U32, name="adj_codes", align_bytes=64
-            )
-            scales = codes_pool.tile(
-                [P, CHUNK_TILES * PASSES * P], U8, name="adj_scales", align_bytes=64
-            )
-            for c in range(CHUNK_TILES):
+        def quantise_adj(b, tiles=range(CHUNK_TILES)):
+            if 0 in tiles:
+                adj_codes.append(
+                    codes_pool.tile(
+                        [P, CHUNK_TILES * PASSES * P], U32, name="adj_codes", align_bytes=64
+                    )
+                )
+                adj_scales.append(
+                    codes_pool.tile(
+                        [P, CHUNK_TILES * PASSES * P], U8, name="adj_scales", align_bytes=64
+                    )
+                )
+            for c in tiles:
+                cols = slice(c * PASSES * P, (c + 1) * PASSES * P)
                 nc.vector.quantize_mx(
-                    out=codes[:, c * PASSES * P : (c + 1) * PASSES * P].bitcast(FP8X4),
-                    scales=scales[:, c * PASSES * P : (c + 1) * PASSES * P],
+                    out=adj_codes[b][:, cols].bitcast(FP8X4),
+                    scales=adj_scales[b][:, cols],
                     in_=adj_grouped[b][:, c * NODES : (c + 1) * NODES],
                 )
-            adj_codes.append(codes)
-            adj_scales.append(scales)
 
-        def multiply_adj(b):
-            out_sum = acc_pool.tile([P, CHUNK_TILES * HID], F32, name="out_sum", tag="acc")
-            for c in range(CHUNK_TILES):
-                for g in range(PASSES):
-                    rows = slice((c * PASSES + g) * P, (c * PASSES + g + 1) * P)
-                    nc.tensor.matmul_mx(
-                        out=out_sum[:, c * HID : (c + 1) * HID],
-                        lhsT=adj_codes[b][:, rows].bitcast(FP8X4),
-                        lhsT_scale=adj_scales[b][:, rows],
-                        rhs=h_codes[:, g * HID : (g + 1) * HID].bitcast(FP8X4),
-                        rhs_scale=h_scales[:, g * HID : (g + 1) * HID],
-                        start=(g == 0),
-                        stop=(g == PASSES - 1),
-                    )
-            result = result_pool.tile([P, CHUNK_TILES * HID], F32, name="result")
+        def multiply_adj(chunks, out_sum):
+            for i in range(len(chunks)):
+                b = chunks[i]
+                for c in range(CHUNK_TILES):
+                    cols = slice((i * CHUNK_TILES + c) * HID, (i * CHUNK_TILES + c + 1) * HID)
+                    for g in range(PASSES):
+                        rows = slice((c * PASSES + g) * P, (c * PASSES + g + 1) * P)
+                        nc.tensor.matmul_mx(
+                            out=out_sum[:, cols],
+                            lhsT=adj_codes[b][:, rows].bitcast(FP8X4),
+                            lhsT_scale=adj_scales[b][:, rows],
+                            rhs=h_codes[:, g * HID : (g + 1) * HID].bitcast(FP8X4),
+                            rhs_scale=h_scales[:, g * HID : (g + 1) * HID],
+                            start=(g == 0),
+                            stop=(g == PASSES - 1),
+                        )
+
+        def finish(chunks, out_sum):
+            width = CHUNK_TILES * HID
+            result = result_pool.tile([P, len(chunks) * width], F32, name="result")
             nc.scalar.activation(
-                out=result[:], in_=out_sum[:], func=mybir.ActivationFunctionType.Relu
+                out=result[:],
+                in_=out_sum[:, : len(chunks) * width],
+                func=mybir.ActivationFunctionType.Relu,
             )
-            nc.sync.dma_start(out=out_view[b], in_=result[:])
+            for i in range(len(chunks)):
+                nc.sync.dma_start(
+                    out=out_view[chunks[i]], in_=result[:, i * width : (i + 1) * width]
+                )
 
-        steps = PASSES + CHUNKS
-        for step in range(steps + LAG):
-            if step < PASSES:
-                flip_x(step)
-            elif step < steps:
-                flip_adj(step - PASSES)
-            if step == 0:
+        def acc_bank():
+            return acc_pool.tile([P, BANK_WORDS], F32, name="out_sum", tag="acc")
+
+        for g in range(PASSES):
+            flip_x(g)
+            if g == 0:
                 spread_bias()
-            ready = step - LAG
-            if 0 <= ready < PASSES:
-                multiply_x(ready)
-            elif ready >= PASSES:
-                multiply_adj(ready - PASSES)
-            if step < PASSES:
-                quantise_x(step)
-            elif step < steps:
-                quantise_adj(step - PASSES)
+            else:
+                quantise_x(g - 1)
+        multiply_x(0)
+        multiply_x(1)
+        add_bias(0)
+        quantise_x(3)
+        add_bias(1)
+        quantise_h(0)
+        quantise_h(1)
+        flip_adj(0)
+        multiply_x(2)
+        multiply_x(3)
+        quantise_adj(0, [0])
+        add_bias(2)
+        quantise_adj(0, [1])
+        add_bias(3)
+        quantise_h(2)
+        quantise_h(3)
+        flip_adj(1)
+        quantise_adj(1)
+        flip_adj(2)
+        quantise_adj(2)
+        flip_adj(3)
+        sum_01 = acc_bank()
+        multiply_adj([0, 1], sum_01)
+        quantise_adj(3)
+        flip_adj(4)
+        finish([0, 1], sum_01)
+        quantise_adj(4)
+        flip_adj(5)
+        sum_23 = acc_bank()
+        multiply_adj([2, 3], sum_23)
+        quantise_adj(5)
+        flip_adj(6)
+        finish([2, 3], sum_23)
+        sum_45 = acc_bank()
+        multiply_adj([4, 5], sum_45)
+        quantise_adj(6)
+        flip_adj(7)
+        finish([4, 5], sum_45)
+        sum_6 = acc_bank()
+        multiply_adj([6], sum_6)
+        finish([6], sum_6)
+        quantise_adj(7)
+        sum_7 = flip_pool.tile([P, BANK_WORDS], F32, name="sum_7", tag="bank")
+        multiply_adj([7], sum_7)
+        finish([7], sum_7)

@@ -22,7 +22,8 @@ CHUNK_TILES = 2
 CHUNKS = NODES // (CHUNK_TILES * P)
 CHUNK_BANKS = CHUNK_TILES * NODES // (2 * BANK_WORDS)
 VECTOR_BANK = 3
-LAST_VECTOR_BANK = 1
+X_V = [(0, 1)]
+A_V = [(0, 3), (1, 3), (2, 3), (3, 3), (4, 3), (5, 3), (6, 3), (7, 1)]
 WARM_UPS = 6
 
 FLOPS = 2 * NODES * FEATS * HID + 2 * NODES * NODES * HID
@@ -40,23 +41,27 @@ def tile_gcn_pa_kernel(tc, x, adj, W0, b0, out):
         ctx.enter_context(tc.manual_schedule())
 
         b_row = keep.tile([1, HID], BF16, name="b_row")
-        nc.sync.dma_start(out=b_row[:], in_=b0.rearrange("(o d) -> o d", o=1))
-
         w_rows = keep.tile([P, PACK, HID], BF16, name="w_rows")
-        nc.scalar.dma_start(
-            out=w_rows[:].rearrange("p (u e) c -> p u (e c)", u=2),
-            in_=W0.rearrange("(u p e) c -> p u (e c)", u=2, e=2),
-        )
-
         x_view = x.rearrange("(c p e) f -> p c (e f)", p=P, e=2)
         x_rows = []
         for g in range(PASSES):
             x_piece = keep.tile([P, PACK * FEATS], BF16, name="x_rows%d" % g)
-            nc.sync.dma_start(
-                out=x_piece[:].rearrange("p (c w) -> p c w", c=2),
-                in_=x_view[:, 2 * g : 2 * g + 2, :],
-            )
+            parts = 2 if g == 0 else 1
+            for part in range(parts):
+                width = PACK * FEATS // parts
+                nc.sync.dma_start(
+                    out=x_piece[:, part * width : (part + 1) * width].rearrange(
+                        "p (c w) -> p c w", c=2 // parts
+                    ),
+                    in_=x_view[:, 2 * g + part : 2 * g + part + 2 // parts, :],
+                )
             x_rows.append(x_piece)
+            if g == 0:
+                nc.sync.dma_start(
+                    out=w_rows[:].rearrange("p (u e) c -> p u (e c)", u=2),
+                    in_=W0.rearrange("(u p e) c -> p u (e c)", u=2, e=2),
+                )
+                nc.sync.dma_start(out=b_row[:], in_=b0.rearrange("(o d) -> o d", o=1))
 
         adj_view = adj.rearrange("(b p c) j -> b p (c j)", p=P, c=CHUNK_TILES)
         out_view = out.rearrange("(b p c) d -> b p (c d)", p=P, c=CHUNK_TILES)
@@ -127,7 +132,11 @@ def tile_gcn_pa_kernel(tc, x, adj, W0, b0, out):
             dst_words = grouped[:].bitcast(F32)
             for k in range(PACK * FEATS // (2 * BANK_WORDS)):
                 words = slice(k * BANK_WORDS, (k + 1) * BANK_WORDS)
-                flip_words(src_words[:, words], dst_words[:, words], nc.scalar.copy)
+                flip_words(
+                    src_words[:, words],
+                    dst_words[:, words],
+                    nc.vector.tensor_copy if (g, k) in X_V else nc.scalar.copy,
+                )
             x_grouped.append(grouped)
 
         def quantise_x(g):
@@ -137,7 +146,10 @@ def tile_gcn_pa_kernel(tc, x, adj, W0, b0, out):
             )
 
         def multiply_x(g):
-            h_sum = acc_pool.tile([P, PACK * HID], F32, name="h_sum", tag="acc")
+            if g < 2:
+                h_sum = acc_pool.tile([P, PACK * HID], F32, name="h_sum", tag="acc")
+            else:
+                h_sum = flip_pool.tile([P, PACK * HID], F32, name="h_sum", tag="bank")
             for t in range(PACK):
                 rows = slice((PACK * g + t) * P, (PACK * g + t + 1) * P)
                 nc.tensor.matmul_mx(
@@ -172,18 +184,20 @@ def tile_gcn_pa_kernel(tc, x, adj, W0, b0, out):
         adj_codes = []
         adj_scales = []
 
-        def flip_adj(b):
-            grouped = grouped_pool.tile(
-                [P, CHUNK_TILES * NODES], BF16, name="adj_grouped", align_bytes=64
-            )
+        def flip_adj(b, banks=range(CHUNK_BANKS)):
+            if 0 in banks:
+                adj_grouped.append(
+                    grouped_pool.tile(
+                        [P, CHUNK_TILES * NODES], BF16, name="adj_grouped", align_bytes=64
+                    )
+                )
+            grouped = adj_grouped[b]
             src_words = adj_rows[b][:].bitcast(F32)
             dst_words = grouped[:].bitcast(F32)
-            for k in range(CHUNK_BANKS):
+            for k in banks:
                 words = slice(k * BANK_WORDS, (k + 1) * BANK_WORDS)
-                mine = LAST_VECTOR_BANK if b == CHUNKS - 1 else VECTOR_BANK
-                copy = nc.vector.tensor_copy if k == mine else nc.scalar.copy
+                copy = nc.vector.tensor_copy if (b, k) in A_V else nc.scalar.copy
                 flip_words(src_words[:, words], dst_words[:, words], copy)
-            adj_grouped.append(grouped)
 
         def quantise_adj(b, tiles=range(CHUNK_TILES)):
             if 0 in tiles:
@@ -238,54 +252,58 @@ def tile_gcn_pa_kernel(tc, x, adj, W0, b0, out):
         def acc_bank():
             return acc_pool.tile([P, BANK_WORDS], F32, name="out_sum", tag="acc")
 
-        for g in range(PASSES):
-            flip_x(g)
-            if g == 0:
-                spread_bias()
-            else:
-                quantise_x(g - 1)
+        flip_x(0)
+        flip_x(1)
+        quantise_x(0)
+        flip_x(2)
+        spread_bias()
+        quantise_x(1)
+        flip_x(3)
+        quantise_x(2)
         multiply_x(0)
         multiply_x(1)
+        multiply_x(2)
         add_bias(0)
         quantise_x(3)
-        add_bias(1)
-        quantise_h(0)
-        quantise_h(1)
-        flip_adj(0)
-        multiply_x(2)
         multiply_x(3)
-        quantise_adj(0, [0])
+        add_bias(1)
         add_bias(2)
-        quantise_adj(0, [1])
+        quantise_h(0)
         add_bias(3)
+        quantise_h(1)
         quantise_h(2)
         quantise_h(3)
+        flip_adj(0)
+        quantise_adj(0)
         flip_adj(1)
+        s0 = acc_bank()
+        multiply_adj([0], s0)
         quantise_adj(1)
         flip_adj(2)
+        finish([0], s0)
         quantise_adj(2)
         flip_adj(3)
-        sum_01 = acc_bank()
-        multiply_adj([0, 1], sum_01)
+        s12 = acc_bank()
+        multiply_adj([1, 2], s12)
         quantise_adj(3)
         flip_adj(4)
-        finish([0, 1], sum_01)
+        s3 = acc_bank()
+        multiply_adj([3], s3)
+        finish([1, 2], s12)
         quantise_adj(4)
         flip_adj(5)
-        sum_23 = acc_bank()
-        multiply_adj([2, 3], sum_23)
         quantise_adj(5)
         flip_adj(6)
-        finish([2, 3], sum_23)
-        sum_45 = acc_bank()
-        multiply_adj([4, 5], sum_45)
+        finish([3], s3)
         quantise_adj(6)
         flip_adj(7)
-        finish([4, 5], sum_45)
-        sum_6 = acc_bank()
-        multiply_adj([6], sum_6)
-        finish([6], sum_6)
+        s45 = acc_bank()
+        multiply_adj([4, 5], s45)
+        finish([4, 5], s45)
+        s6 = acc_bank()
+        multiply_adj([6], s6)
+        finish([6], s6)
         quantise_adj(7)
-        sum_7 = flip_pool.tile([P, BANK_WORDS], F32, name="sum_7", tag="bank")
-        multiply_adj([7], sum_7)
-        finish([7], sum_7)
+        s7 = flip_pool.tile([P, BANK_WORDS], F32, name="s7", tag="bank")
+        multiply_adj([7], s7)
+        finish([7], s7)

@@ -24,6 +24,7 @@ CHUNK_BANKS = CHUNK_TILES * NODES // (2 * BANK_WORDS)
 VECTOR_BANK = 3
 X_V = [(0, 1)]
 A_V = [(0, 3), (1, 3), (2, 3), (3, 3), (4, 3), (5, 3), (6, 3), (7, 1)]
+SPLIT_FROM = 0
 WARM_UPS = 6
 
 FLOPS = 2 * NODES * FEATS * HID + 2 * NODES * NODES * HID
@@ -68,10 +69,15 @@ def tile_gcn_pa_kernel(tc, x, adj, W0, b0, out):
         adj_rows = []
         for b in range(CHUNKS):
             adj_piece = keep.tile([P, CHUNK_TILES * NODES], BF16, name="adj_rows%d" % b)
-            parts = 2 if b == CHUNKS - 1 else 1
-            for part in range(parts):
-                width = CHUNK_TILES * NODES // parts
-                cols = slice(part * width, (part + 1) * width)
+            widths = (
+                [NODES, NODES // 2, NODES // 2]
+                if b == CHUNKS - 1
+                else [NODES] * 2
+                if b >= SPLIT_FROM
+                else [2 * NODES]
+            )
+            for i in range(len(widths)):
+                cols = slice(sum(widths[:i]), sum(widths[: i + 1]))
                 nc.sync.dma_start(out=adj_piece[:, cols], in_=adj_view[b][:, cols])
             adj_rows.append(adj_piece)
 
@@ -80,13 +86,13 @@ def tile_gcn_pa_kernel(tc, x, adj, W0, b0, out):
 
         ones = keep.tile([P, P], BF16, name="ones")
         nc.vector.memset(ones[:], 1.0)
-        zeros = keep.tile([P, BANK_WORDS], BF16, name="zeros")
-        nc.vector.memset(zeros[:], 0.0)
         b_rows = keep.tile([P, HID], BF16, name="b_rows")
         nc.vector.memset(b_rows[:], 0.0)
         idle_sum = flip_pool.tile([P, BANK_WORDS], F32, name="idle_sum", tag="bank")
         for warm_up in range(WARM_UPS):
-            nc.tensor.matmul(out=idle_sum[:], lhsT=ones[:], rhs=zeros[:], start=True, stop=True)
+            nc.tensor.matmul(
+                out=idle_sum[:, :P], lhsT=ident[:], rhs=ident[:], start=True, stop=True
+            )
 
         bias = keep.tile([P, HID], F32, name="bias")
 
@@ -108,8 +114,12 @@ def tile_gcn_pa_kernel(tc, x, adj, W0, b0, out):
             in_=w_grouped[:].rearrange("p c t -> p (c t)"),
         )
 
-        def flip_words(src_words, dst_words, copy):
+        def flip_words(src_words, dst_words, copy, warm=False):
             bank = flip_pool.tile([P, BANK_WORDS], F32, name="bank", tag="bank")
+            if warm:
+                nc.tensor.matmul(
+                    out=bank[:, :P], lhsT=ident[:], rhs=ident[:], start=True, stop=True
+                )
             for q in range(BANK_WORDS // P):
                 cols = slice(q * P, (q + 1) * P)
                 nc.tensor.transpose(bank[:, cols], src_words[:, cols], ident[:])
@@ -126,7 +136,7 @@ def tile_gcn_pa_kernel(tc, x, adj, W0, b0, out):
         h_codes = keep.tile([P, PASSES * HID], U32, name="h_codes", align_bytes=64)
         h_scales = keep.tile([P, PASSES * HID], U8, name="h_scales", align_bytes=64)
 
-        def flip_x(g):
+        def flip_x(g, warm=False):
             grouped = keep.tile([P, PACK * FEATS], BF16, name="x_grouped%d" % g, align_bytes=64)
             src_words = x_rows[g][:].bitcast(F32)
             dst_words = grouped[:].bitcast(F32)
@@ -136,6 +146,7 @@ def tile_gcn_pa_kernel(tc, x, adj, W0, b0, out):
                     src_words[:, words],
                     dst_words[:, words],
                     nc.vector.tensor_copy if (g, k) in X_V else nc.scalar.copy,
+                    warm and k == 1,
                 )
             x_grouped.append(grouped)
 
@@ -184,7 +195,7 @@ def tile_gcn_pa_kernel(tc, x, adj, W0, b0, out):
         adj_codes = []
         adj_scales = []
 
-        def flip_adj(b, banks=range(CHUNK_BANKS)):
+        def flip_adj(b, banks=range(CHUNK_BANKS), warm=False):
             if 0 in banks:
                 adj_grouped.append(
                     grouped_pool.tile(
@@ -197,57 +208,81 @@ def tile_gcn_pa_kernel(tc, x, adj, W0, b0, out):
             for k in banks:
                 words = slice(k * BANK_WORDS, (k + 1) * BANK_WORDS)
                 copy = nc.vector.tensor_copy if (b, k) in A_V else nc.scalar.copy
-                flip_words(src_words[:, words], dst_words[:, words], copy)
+                flip_words(
+                    src_words[:, words], dst_words[:, words], copy, warm and k == CHUNK_BANKS - 1
+                )
 
-        def quantise_adj(b, tiles=range(CHUNK_TILES)):
-            if 0 in tiles:
-                adj_codes.append(
-                    codes_pool.tile(
-                        [P, CHUNK_TILES * PASSES * P], U32, name="adj_codes", align_bytes=64
-                    )
-                )
-                adj_scales.append(
-                    codes_pool.tile(
-                        [P, CHUNK_TILES * PASSES * P], U8, name="adj_scales", align_bytes=64
-                    )
-                )
-            for c in tiles:
-                cols = slice(c * PASSES * P, (c + 1) * PASSES * P)
+        def quantise_adj(b, parts=((0, 4), (4, 8))):
+            if parts[0][0] == 0:
+                width = CHUNK_TILES * PASSES * P
+                adj_codes.append(codes_pool.tile([P, width], U32, name="adj_codes", align_bytes=64))
+                adj_scales.append(codes_pool.tile([P, width], U8, name="adj_scales", align_bytes=64))
+            for first, end in parts:
+                cols = slice(first * P, end * P)
                 nc.vector.quantize_mx(
                     out=adj_codes[b][:, cols].bitcast(FP8X4),
                     scales=adj_scales[b][:, cols],
-                    in_=adj_grouped[b][:, c * NODES : (c + 1) * NODES],
+                    in_=adj_grouped[b][:, first * K_PASS : end * K_PASS],
+                )
+
+        def multiply_tile(b, c, sums, passes=range(PASSES)):
+            for g in passes:
+                rows = slice((c * PASSES + g) * P, (c * PASSES + g + 1) * P)
+                nc.tensor.matmul_mx(
+                    out=sums,
+                    lhsT=adj_codes[b][:, rows].bitcast(FP8X4),
+                    lhsT_scale=adj_scales[b][:, rows],
+                    rhs=h_codes[:, g * HID : (g + 1) * HID].bitcast(FP8X4),
+                    rhs_scale=h_scales[:, g * HID : (g + 1) * HID],
+                    start=(g == 0),
+                    stop=(g == PASSES - 1),
                 )
 
         def multiply_adj(chunks, out_sum):
             for i in range(len(chunks)):
-                b = chunks[i]
                 for c in range(CHUNK_TILES):
-                    cols = slice((i * CHUNK_TILES + c) * HID, (i * CHUNK_TILES + c + 1) * HID)
-                    for g in range(PASSES):
-                        rows = slice((c * PASSES + g) * P, (c * PASSES + g + 1) * P)
-                        nc.tensor.matmul_mx(
-                            out=out_sum[:, cols],
-                            lhsT=adj_codes[b][:, rows].bitcast(FP8X4),
-                            lhsT_scale=adj_scales[b][:, rows],
-                            rhs=h_codes[:, g * HID : (g + 1) * HID].bitcast(FP8X4),
-                            rhs_scale=h_scales[:, g * HID : (g + 1) * HID],
-                            start=(g == 0),
-                            stop=(g == PASSES - 1),
-                        )
+                    tile = i * CHUNK_TILES + c
+                    multiply_tile(chunks[i], c, out_sum[:, tile * HID : (tile + 1) * HID])
 
-        def finish(chunks, out_sum):
+        def finish(chunks, out_sum, eng='s'):
             width = CHUNK_TILES * HID
             result = result_pool.tile([P, len(chunks) * width], F32, name="result")
-            nc.scalar.activation(
-                out=result[:],
-                in_=out_sum[:, : len(chunks) * width],
-                func=mybir.ActivationFunctionType.Relu,
-            )
+            relu(result[:], out_sum[:, : len(chunks) * width], eng)
             for i in range(len(chunks)):
                 nc.sync.dma_start(
                     out=out_view[chunks[i]], in_=result[:, i * width : (i + 1) * width]
                 )
+
+        def relu(out, in_, eng='s'):
+            if eng == 's':
+                nc.scalar.activation(out=out, in_=in_, func=mybir.ActivationFunctionType.Relu)
+            else:
+                nc.vector.tensor_scalar_max(out=out, in0=in_, scalar1=0.0)
+
+        def finish_tile(b, c, out_sum, eng='s'):
+            result = result_pool.tile([P, HID], F32, name="result_tile")
+            relu(result[:], out_sum[:, :HID], eng)
+            nc.sync.dma_start(out=out_view[b][:, c * HID : (c + 1) * HID], in_=result[:])
+
+        def flip_last():
+            src_words = adj_rows[CHUNKS - 1][:].bitcast(F32)
+            dst_words = adj_grouped[CHUNKS - 1][:].bitcast(F32)
+            for half in range(2):
+                copy = [nc.scalar.copy, nc.vector.tensor_copy][half]
+                bank = flip_pool.tile([P, BANK_WORDS], F32, name="bank", tag="bank")
+                first = (CHUNK_BANKS - 1) * BANK_WORDS + half * 2 * P
+                for q in range(2):
+                    cols = slice(q * P, (q + 1) * P)
+                    nc.tensor.transpose(
+                        bank[:, cols], src_words[:, first + q * P : first + (q + 1) * P], ident[:]
+                    )
+                copy(
+                    out=dst_words[:, first : first + 2 * P].rearrange("p (r u) -> p r u", u=2),
+                    in_=bank[:, : 2 * P].rearrange("p (u r) -> p r u", u=2),
+                )
+
+        def flip_bank():
+            return flip_pool.tile([P, BANK_WORDS], F32, name="last_sum", tag="bank")
 
         def acc_bank():
             return acc_pool.tile([P, BANK_WORDS], F32, name="out_sum", tag="acc")
@@ -273,37 +308,57 @@ def tile_gcn_pa_kernel(tc, x, adj, W0, b0, out):
         quantise_h(1)
         quantise_h(2)
         quantise_h(3)
-        flip_adj(0)
-        quantise_adj(0)
-        flip_adj(1)
+        flip_adj(0, [0, 1])
+        flip_adj(0, [2, 3])
+        quantise_adj(0, [(0, 4)])
+        flip_adj(1, [0, 1])
+        quantise_adj(0, [(4, 8)])
+        flip_adj(1, [2, 3])
+        quantise_adj(1, [(0, 4)])
+        flip_adj(2, [0, 1])
+        quantise_adj(1, [(4, 8)])
+        flip_adj(2, [2, 3])
         s0 = acc_bank()
-        multiply_adj([0], s0)
-        quantise_adj(1)
-        flip_adj(2)
-        finish([0], s0)
-        quantise_adj(2)
-        flip_adj(3)
-        s12 = acc_bank()
-        multiply_adj([1, 2], s12)
-        quantise_adj(3)
-        flip_adj(4)
+        multiply_adj([0, 1], s0)
+        quantise_adj(2, [(0, 4)])
+        flip_adj(3, [0, 1])
+        quantise_adj(2, [(4, 8)])
+        flip_adj(3, [2, 3])
+        quantise_adj(3, [(0, 4)])
+        finish([0, 1], s0, 's')
+        flip_adj(4, [0, 1])
+        quantise_adj(3, [(4, 8)])
+        flip_adj(4, [2, 3])
+        s2 = acc_bank()
+        multiply_adj([2], s2)
+        quantise_adj(4, [(0, 4)])
+        flip_adj(5, [0, 1])
+        quantise_adj(4, [(4, 8)])
+        flip_adj(5, [2, 3])
         s3 = acc_bank()
         multiply_adj([3], s3)
-        finish([1, 2], s12)
-        quantise_adj(4)
-        flip_adj(5)
-        quantise_adj(5)
-        flip_adj(6)
-        finish([3], s3)
-        quantise_adj(6)
-        flip_adj(7)
+        quantise_adj(5, [(0, 4)])
+        finish([2], s2, 's')
+        flip_adj(6, [0, 1])
+        quantise_adj(5, [(4, 8)])
+        flip_adj(6, [2, 3])
+        quantise_adj(6, [(0, 4)])
+        finish([3], s3, 's')
+        flip_adj(7, [0, 1])
+        quantise_adj(6, [(4, 8)])
+        flip_adj(7, [2])
+        quantise_adj(7, [(0, 4)])
+        flip_last()
+        quantise_adj(7, [(4, 6), (6, 7), (7, 8)])
         s45 = acc_bank()
         multiply_adj([4, 5], s45)
-        finish([4, 5], s45)
+        finish([4, 5], s45, 's')
         s6 = acc_bank()
         multiply_adj([6], s6)
-        finish([6], s6)
-        quantise_adj(7)
-        s7 = flip_pool.tile([P, BANK_WORDS], F32, name="s7", tag="bank")
-        multiply_adj([7], s7)
-        finish([7], s7)
+        finish([6], s6, 's')
+        s14 = flip_bank()
+        multiply_tile(7, 0, s14[:, :HID])
+        finish_tile(7, 0, s14)
+        s15 = flip_bank()
+        multiply_tile(7, 1, s15[:, :HID])
+        finish_tile(7, 1, s15)

@@ -23,9 +23,11 @@ CHUNKS = NODES // (CHUNK_TILES * P)
 CHUNK_BANKS = CHUNK_TILES * NODES // (2 * BANK_WORDS)
 VECTOR_BANK = 3
 X_V = [(0, 1)]
-A_V = [(0, 3), (1, 3), (2, 3), (3, 3), (4, 3), (5, 3), (6, 3), (7, 1)]
+A_V = [(0, 3), (1, 3), (2, 3), (3, 3), (4, 3), (5, 3), (6, 1), (7, 1)]
 SPLIT_FROM = 0
-WARM_UPS = 6
+W_AFTER = 0
+X_HALVES = (0,)
+WARM_UPS = 3
 
 FLOPS = 2 * NODES * FEATS * HID + 2 * NODES * NODES * HID
 
@@ -47,7 +49,7 @@ def tile_gcn_pa_kernel(tc, x, adj, W0, b0, out):
         x_rows = []
         for g in range(PASSES):
             x_piece = keep.tile([P, PACK * FEATS], BF16, name="x_rows%d" % g)
-            parts = 2 if g == 0 else 1
+            parts = 2 if g in X_HALVES else 1
             for part in range(parts):
                 width = PACK * FEATS // parts
                 nc.sync.dma_start(
@@ -57,7 +59,7 @@ def tile_gcn_pa_kernel(tc, x, adj, W0, b0, out):
                     in_=x_view[:, 2 * g + part : 2 * g + part + 2 // parts, :],
                 )
             x_rows.append(x_piece)
-            if g == 0:
+            if g == W_AFTER:
                 nc.sync.dma_start(
                     out=w_rows[:].rearrange("p (u e) c -> p u (e c)", u=2),
                     in_=W0.rearrange("(u p e) c -> p u (e c)", u=2, e=2),
@@ -105,14 +107,18 @@ def tile_gcn_pa_kernel(tc, x, adj, W0, b0, out):
             )
 
         w_grouped = keep.tile([P, HID, PACK], BF16, name="w_grouped", align_bytes=64)
-        nc.vector.tensor_copy(out=w_grouped[:], in_=w_rows[:].rearrange("p t c -> p c t"))
         w_codes = keep.tile([P, HID], U32, name="w_codes", align_bytes=64)
         w_scales = keep.tile([P, HID], U8, name="w_scales", align_bytes=64)
-        nc.vector.quantize_mx(
-            out=w_codes[:].bitcast(FP8X4),
-            scales=w_scales[:],
-            in_=w_grouped[:].rearrange("p c t -> p (c t)"),
-        )
+
+        def group_w():
+            nc.vector.tensor_copy(out=w_grouped[:], in_=w_rows[:].rearrange("p t c -> p c t"))
+
+        def quantise_w():
+            nc.vector.quantize_mx(
+                out=w_codes[:].bitcast(FP8X4),
+                scales=w_scales[:],
+                in_=w_grouped[:].rearrange("p c t -> p (c t)"),
+            )
 
         def flip_words(src_words, dst_words, copy, warm=False):
             bank = flip_pool.tile([P, BANK_WORDS], F32, name="bank", tag="bank")
@@ -146,7 +152,7 @@ def tile_gcn_pa_kernel(tc, x, adj, W0, b0, out):
                     src_words[:, words],
                     dst_words[:, words],
                     nc.vector.tensor_copy if (g, k) in X_V else nc.scalar.copy,
-                    warm and k == 1,
+                    warm and k == 0,
                 )
             x_grouped.append(grouped)
 
@@ -209,7 +215,7 @@ def tile_gcn_pa_kernel(tc, x, adj, W0, b0, out):
                 words = slice(k * BANK_WORDS, (k + 1) * BANK_WORDS)
                 copy = nc.vector.tensor_copy if (b, k) in A_V else nc.scalar.copy
                 flip_words(
-                    src_words[:, words], dst_words[:, words], copy, warm and k == CHUNK_BANKS - 1
+                    src_words[:, words], dst_words[:, words], copy, warm and k == banks[0]
                 )
 
         def quantise_adj(b, parts=((0, 4), (4, 8))):
@@ -238,11 +244,10 @@ def tile_gcn_pa_kernel(tc, x, adj, W0, b0, out):
                     stop=(g == PASSES - 1),
                 )
 
-        def multiply_adj(chunks, out_sum):
-            for i in range(len(chunks)):
-                for c in range(CHUNK_TILES):
-                    tile = i * CHUNK_TILES + c
-                    multiply_tile(chunks[i], c, out_sum[:, tile * HID : (tile + 1) * HID])
+        def multiply_tiles(tiles, out_sum, first):
+            for tile in tiles:
+                cols = slice((tile - first) * HID, (tile - first + 1) * HID)
+                multiply_tile(tile // CHUNK_TILES, tile % CHUNK_TILES, out_sum[:, cols])
 
         def finish(chunks, out_sum, eng='s'):
             width = CHUNK_TILES * HID
@@ -287,18 +292,21 @@ def tile_gcn_pa_kernel(tc, x, adj, W0, b0, out):
         def acc_bank():
             return acc_pool.tile([P, BANK_WORDS], F32, name="out_sum", tag="acc")
 
+        group_w()
+        quantise_w()
         flip_x(0)
-        flip_x(1)
+        flip_x(1, warm=True)
         quantise_x(0)
-        flip_x(2)
+        flip_x(2, warm=True)
         spread_bias()
         quantise_x(1)
-        flip_x(3)
+        flip_x(3, warm=True)
         quantise_x(2)
         multiply_x(0)
         multiply_x(1)
         multiply_x(2)
         add_bias(0)
+        flip_adj(0, [0, 1])
         quantise_x(3)
         multiply_x(3)
         add_bias(1)
@@ -308,54 +316,54 @@ def tile_gcn_pa_kernel(tc, x, adj, W0, b0, out):
         quantise_h(1)
         quantise_h(2)
         quantise_h(3)
-        flip_adj(0, [0, 1])
-        flip_adj(0, [2, 3])
+        flip_adj(0, [2, 3], warm=True)
         quantise_adj(0, [(0, 4)])
-        flip_adj(1, [0, 1])
+        flip_adj(1, [0, 1], warm=True)
         quantise_adj(0, [(4, 8)])
-        flip_adj(1, [2, 3])
+        flip_adj(1, [2, 3], warm=True)
         quantise_adj(1, [(0, 4)])
         flip_adj(2, [0, 1])
         quantise_adj(1, [(4, 8)])
         flip_adj(2, [2, 3])
-        s0 = acc_bank()
-        multiply_adj([0, 1], s0)
+        g0 = acc_bank()
+        multiply_tiles([0, 1, 2], g0, 0)
         quantise_adj(2, [(0, 4)])
         flip_adj(3, [0, 1])
         quantise_adj(2, [(4, 8)])
         flip_adj(3, [2, 3])
+        multiply_tiles([3], g0, 0)
+        g1 = acc_bank()
+        multiply_tiles([4], g1, 4)
         quantise_adj(3, [(0, 4)])
-        finish([0, 1], s0, 's')
         flip_adj(4, [0, 1])
         quantise_adj(3, [(4, 8)])
         flip_adj(4, [2, 3])
-        s2 = acc_bank()
-        multiply_adj([2], s2)
+        multiply_tiles([5, 6], g1, 4)
         quantise_adj(4, [(0, 4)])
+        finish([0, 1], g0, 's')
         flip_adj(5, [0, 1])
         quantise_adj(4, [(4, 8)])
         flip_adj(5, [2, 3])
-        s3 = acc_bank()
-        multiply_adj([3], s3)
+        multiply_tiles([7], g1, 4)
+        g2 = acc_bank()
+        multiply_tiles([8], g2, 8)
         quantise_adj(5, [(0, 4)])
-        finish([2], s2, 's')
         flip_adj(6, [0, 1])
         quantise_adj(5, [(4, 8)])
         flip_adj(6, [2, 3])
         quantise_adj(6, [(0, 4)])
-        finish([3], s3, 's')
+        finish([2, 3], g1, 's')
         flip_adj(7, [0, 1])
         quantise_adj(6, [(4, 8)])
         flip_adj(7, [2])
         quantise_adj(7, [(0, 4)])
         flip_last()
         quantise_adj(7, [(4, 6), (6, 7), (7, 8)])
-        s45 = acc_bank()
-        multiply_adj([4, 5], s45)
-        finish([4, 5], s45, 's')
-        s6 = acc_bank()
-        multiply_adj([6], s6)
-        finish([6], s6, 's')
+        multiply_tiles([9, 10, 11], g2, 8)
+        finish([4, 5], g2, 's')
+        g3 = acc_bank()
+        multiply_tiles([12, 13], g3, 12)
+        finish([6], g3, 's')
         s14 = flip_bank()
         multiply_tile(7, 0, s14[:, :HID])
         finish_tile(7, 0, s14)

from contextlib import ExitStack

import concourse.mybir as mybir
from concourse.masks import make_identity

F32 = mybir.dt.float32
BF16 = mybir.dt.bfloat16
U32 = mybir.dt.uint32
U8 = mybir.dt.uint8
FP8X4 = mybir.dt.float8_e4m3fn_x4

P = 128
PACK = 4
K_PASS = P * PACK
BANK_WORDS = 512

NODES = 2048
FEATS = 512
HID = 128
PASSES = NODES // K_PASS
CHUNK_TILES = 2
CHUNKS = NODES // (CHUNK_TILES * P)
CHUNK_BANKS = CHUNK_TILES * NODES // (2 * BANK_WORDS)
VECTOR_BANK = 3
X_V = [(0, 1)]
A_V = [(0, 3), (1, 3), (2, 3), (3, 3), (4, 3), (5, 3), (6, 1), (7, 1)]
SPLIT_FROM = 0
W_AFTER = 0
X_HALVES = (0,)
WARM_UPS = 3

FLOPS = 2 * NODES * FEATS * HID + 2 * NODES * NODES * HID


def tile_gcn_pa_kernel(tc, x, adj, W0, b0, out):
    nc = tc.nc
    with ExitStack() as ctx:
        keep = ctx.enter_context(tc.tile_pool(name="keep", bufs=1))
        grouped_pool = ctx.enter_context(tc.tile_pool(name="grouped", bufs=4))
        codes_pool = ctx.enter_context(tc.tile_pool(name="codes", bufs=6))
        result_pool = ctx.enter_context(tc.tile_pool(name="result", bufs=4))
        flip_pool = ctx.enter_context(tc.psum_pool(name="flip", bufs=6))
        acc_pool = ctx.enter_context(tc.psum_pool(name="acc", bufs=2))
        ctx.enter_context(tc.manual_schedule())

        b_row = keep.tile([1, HID], BF16, name="b_row")
        w_rows = keep.tile([P, PACK, HID], BF16, name="w_rows")
        x_view = x.rearrange("(c p e) f -> p c (e f)", p=P, e=2)
        x_rows = []
        for g in range(PASSES):
            x_piece = keep.tile([P, PACK * FEATS], BF16, name="x_rows%d" % g)
            parts = 2 if g in X_HALVES else 1
            for part in range(parts):
                width = PACK * FEATS // parts
                nc.sync.dma_start(
                    out=x_piece[:, part * width : (part + 1) * width].rearrange(
                        "p (c w) -> p c w", c=2 // parts
                    ),
                    in_=x_view[:, 2 * g + part : 2 * g + part + 2 // parts, :],
                )
            x_rows.append(x_piece)
            if g == W_AFTER:
                nc.sync.dma_start(
                    out=w_rows[:].rearrange("p (u e) c -> p u (e c)", u=2),
                    in_=W0.rearrange("(u p e) c -> p u (e c)", u=2, e=2),
                )
                nc.sync.dma_start(out=b_row[:], in_=b0.rearrange("(o d) -> o d", o=1))

        adj_view = adj.rearrange("(b p c) j -> b p (c j)", p=P, c=CHUNK_TILES)
        out_view = out.rearrange("(b p c) d -> b p (c d)", p=P, c=CHUNK_TILES)
        adj_rows = []
        for b in range(CHUNKS):
            adj_piece = keep.tile([P, CHUNK_TILES * NODES], BF16, name="adj_rows%d" % b)
            widths = (
                [NODES, NODES // 2, NODES // 2]
                if b == CHUNKS - 1
                else [NODES] * 2
                if b >= SPLIT_FROM
                else [2 * NODES]
            )
            for i in range(len(widths)):
                cols = slice(sum(widths[:i]), sum(widths[: i + 1]))
                nc.sync.dma_start(out=adj_piece[:, cols], in_=adj_view[b][:, cols])
            adj_rows.append(adj_piece)

        ident = keep.tile([P, P], F32, name="ident")
        make_identity(nc, ident[:])

        ones = keep.tile([P, P], BF16, name="ones")
        nc.vector.memset(ones[:], 1.0)
        b_rows = keep.tile([P, HID], BF16, name="b_rows")
        nc.vector.memset(b_rows[:], 0.0)
        idle_sum = flip_pool.tile([P, BANK_WORDS], F32, name="idle_sum", tag="bank")
        for warm_up in range(WARM_UPS):
            nc.tensor.matmul(
                out=idle_sum[:, :P], lhsT=ident[:], rhs=ident[:], start=True, stop=True
            )

        bias = keep.tile([P, HID], F32, name="bias")

        def spread_bias():
            nc.vector.tensor_copy(out=b_rows[0:1, :], in_=b_row[:])
            bias_sum = acc_pool.tile([P, HID], F32, name="bias_sum", tag="acc")
            nc.tensor.matmul(out=bias_sum[:], lhsT=ones[:], rhs=b_rows[:], start=True, stop=True)
            nc.scalar.activation(
                out=bias[:], in_=bias_sum[:], func=mybir.ActivationFunctionType.Copy
            )

        w_grouped = keep.tile([P, HID, PACK], BF16, name="w_grouped", align_bytes=64)
        w_codes = keep.tile([P, HID], U32, name="w_codes", align_bytes=64)
        w_scales = keep.tile([P, HID], U8, name="w_scales", align_bytes=64)

        def group_w():
            nc.vector.tensor_copy(out=w_grouped[:], in_=w_rows[:].rearrange("p t c -> p c t"))

        def quantise_w():
            nc.vector.quantize_mx(
                out=w_codes[:].bitcast(FP8X4),
                scales=w_scales[:],
                in_=w_grouped[:].rearrange("p c t -> p (c t)"),
            )

        def flip_words(src_words, dst_words, copy, warm=False):
            bank = flip_pool.tile([P, BANK_WORDS], F32, name="bank", tag="bank")
            if warm:
                nc.tensor.matmul(
                    out=bank[:, :P], lhsT=ident[:], rhs=ident[:], start=True, stop=True
                )
            for q in range(BANK_WORDS // P):
                cols = slice(q * P, (q + 1) * P)
                nc.tensor.transpose(bank[:, cols], src_words[:, cols], ident[:])
            copy(
                out=dst_words.rearrange("p (a r u) -> p a r u", a=2, u=2),
                in_=bank[:].rearrange("p (a u r) -> p a r u", a=2, u=2),
            )

        x_grouped = []
        h_sums = []
        x_codes = keep.tile([P, PASSES * K_PASS], U32, name="x_codes", align_bytes=64)
        x_scales = keep.tile([P, PASSES * K_PASS], U8, name="x_scales", align_bytes=64)
        h_grouped = keep.tile([P, PASSES * HID * PACK], BF16, name="h_grouped", align_bytes=64)
        h_codes = keep.tile([P, PASSES * HID], U32, name="h_codes", align_bytes=64)
        h_scales = keep.tile([P, PASSES * HID], U8, name="h_scales", align_bytes=64)

        def flip_x(g, warm=False):
            grouped = keep.tile([P, PACK * FEATS], BF16, name="x_grouped%d" % g, align_bytes=64)
            src_words = x_rows[g][:].bitcast(F32)
            dst_words = grouped[:].bitcast(F32)
            for k in range(PACK * FEATS // (2 * BANK_WORDS)):
                words = slice(k * BANK_WORDS, (k + 1) * BANK_WORDS)
                flip_words(
                    src_words[:, words],
                    dst_words[:, words],
                    nc.vector.tensor_copy if (g, k) in X_V else nc.scalar.copy,
                    warm and k == 0,
                )
            x_grouped.append(grouped)

        def quantise_x(g):
            cols = slice(g * K_PASS, (g + 1) * K_PASS)
            nc.vector.quantize_mx(
                out=x_codes[:, cols].bitcast(FP8X4), scales=x_scales[:, cols], in_=x_grouped[g][:]
            )

        def multiply_x(g):
            if g < 2:
                h_sum = acc_pool.tile([P, PACK * HID], F32, name="h_sum", tag="acc")
            else:
                h_sum = flip_pool.tile([P, PACK * HID], F32, name="h_sum", tag="bank")
            for t in range(PACK):
                rows = slice((PACK * g + t) * P, (PACK * g + t + 1) * P)
                nc.tensor.matmul_mx(
                    out=h_sum[:, t * HID : (t + 1) * HID],
                    lhsT=x_codes[:, rows].bitcast(FP8X4),
                    lhsT_scale=x_scales[:, rows],
                    rhs=w_codes[:].bitcast(FP8X4),
                    rhs_scale=w_scales[:],
                    start=True,
                    stop=True,
                )
            h_sums.append(h_sum)

        def add_bias(g):
            cols = slice(g * HID * PACK, (g + 1) * HID * PACK)
            nc.vector.tensor_tensor(
                out=h_grouped[:, cols].rearrange("p (d t) -> p d t", t=PACK),
                in0=h_sums[g][:].rearrange("p (t d) -> p d t", t=PACK),
                in1=bias[:].unsqueeze(2).to_broadcast([P, HID, PACK]),
                op=mybir.AluOpType.add,
            )

        def quantise_h(g):
            cols = slice(g * HID * PACK, (g + 1) * HID * PACK)
            nc.vector.quantize_mx(
                out=h_codes[:, g * HID : (g + 1) * HID].bitcast(FP8X4),
                scales=h_scales[:, g * HID : (g + 1) * HID],
                in_=h_grouped[:, cols],
            )

        adj_grouped = []
        adj_codes = []
        adj_scales = []

        def flip_adj(b, banks=range(CHUNK_BANKS), warm=False):
            if 0 in banks:
                adj_grouped.append(
                    grouped_pool.tile(
                        [P, CHUNK_TILES * NODES], BF16, name="adj_grouped", align_bytes=64
                    )
                )
            grouped = adj_grouped[b]
            src_words = adj_rows[b][:].bitcast(F32)
            dst_words = grouped[:].bitcast(F32)
            for k in banks:
                words = slice(k * BANK_WORDS, (k + 1) * BANK_WORDS)
                copy = nc.vector.tensor_copy if (b, k) in A_V else nc.scalar.copy
                flip_words(
                    src_words[:, words], dst_words[:, words], copy, warm and k == banks[0]
                )

        def quantise_adj(b, parts=((0, 4), (4, 8))):
            if parts[0][0] == 0:
                width = CHUNK_TILES * PASSES * P
                adj_codes.append(codes_pool.tile([P, width], U32, name="adj_codes", align_bytes=64))
                adj_scales.append(codes_pool.tile([P, width], U8, name="adj_scales", align_bytes=64))
            for first, end in parts:
                cols = slice(first * P, end * P)
                nc.vector.quantize_mx(
                    out=adj_codes[b][:, cols].bitcast(FP8X4),
                    scales=adj_scales[b][:, cols],
                    in_=adj_grouped[b][:, first * K_PASS : end * K_PASS],
                )

        def multiply_tile(b, c, sums, passes=range(PASSES)):
            for g in passes:
                rows = slice((c * PASSES + g) * P, (c * PASSES + g + 1) * P)
                nc.tensor.matmul_mx(
                    out=sums,
                    lhsT=adj_codes[b][:, rows].bitcast(FP8X4),
                    lhsT_scale=adj_scales[b][:, rows],
                    rhs=h_codes[:, g * HID : (g + 1) * HID].bitcast(FP8X4),
                    rhs_scale=h_scales[:, g * HID : (g + 1) * HID],
                    start=(g == 0),
                    stop=(g == PASSES - 1),
                )

        def multiply_tiles(tiles, out_sum, first):
            for tile in tiles:
                cols = slice((tile - first) * HID, (tile - first + 1) * HID)
                multiply_tile(tile // CHUNK_TILES, tile % CHUNK_TILES, out_sum[:, cols])

        def finish(chunks, out_sum, eng='s'):
            width = CHUNK_TILES * HID
            result = result_pool.tile([P, len(chunks) * width], F32, name="result")
            relu(result[:], out_sum[:, : len(chunks) * width], eng)
            for i in range(len(chunks)):
                nc.sync.dma_start(
                    out=out_view[chunks[i]], in_=result[:, i * width : (i + 1) * width]
                )

        def relu(out, in_, eng='s'):
            if eng == 's':
                nc.scalar.activation(out=out, in_=in_, func=mybir.ActivationFunctionType.Relu)
            else:
                nc.vector.tensor_scalar_max(out=out, in0=in_, scalar1=0.0)

        def finish_tile(b, c, out_sum, eng='s'):
            result = result_pool.tile([P, HID], F32, name="result_tile")
            relu(result[:], out_sum[:, :HID], eng)
            nc.sync.dma_start(out=out_view[b][:, c * HID : (c + 1) * HID], in_=result[:])

        def flip_last():
            src_words = adj_rows[CHUNKS - 1][:].bitcast(F32)
            dst_words = adj_grouped[CHUNKS - 1][:].bitcast(F32)
            for half in range(2):
                copy = [nc.scalar.copy, nc.vector.tensor_copy][half]
                bank = flip_pool.tile([P, BANK_WORDS], F32, name="bank", tag="bank")
                first = (CHUNK_BANKS - 1) * BANK_WORDS + half * 2 * P
                for q in range(2):
                    cols = slice(q * P, (q + 1) * P)
                    nc.tensor.transpose(
                        bank[:, cols], src_words[:, first + q * P : first + (q + 1) * P], ident[:]
                    )
                copy(
                    out=dst_words[:, first : first + 2 * P].rearrange("p (r u) -> p r u", u=2),
                    in_=bank[:, : 2 * P].rearrange("p (u r) -> p r u", u=2),
                )

        def flip_bank():
            return flip_pool.tile([P, BANK_WORDS], F32, name="last_sum", tag="bank")

        def acc_bank():
            return acc_pool.tile([P, BANK_WORDS], F32, name="out_sum", tag="acc")

        group_w()
        quantise_w()
        flip_x(0)
        flip_x(1, warm=True)
        quantise_x(0)
        flip_x(2, warm=True)
        spread_bias()
        quantise_x(1)
        flip_x(3, warm=True)
        quantise_x(2)
        multiply_x(0)
        multiply_x(1)
        multiply_x(2)
        add_bias(0)
        flip_adj(0, [0, 1])
        quantise_x(3)
        multiply_x(3)
        add_bias(1)
        add_bias(2)
        quantise_h(0)
        add_bias(3)
        quantise_h(1)
        quantise_h(2)
        quantise_h(3)
        flip_adj(0, [2, 3], warm=True)
        quantise_adj(0, [(0, 4)])
        flip_adj(1, [0, 1], warm=True)
        quantise_adj(0, [(4, 8)])
        flip_adj(1, [2, 3], warm=True)
        quantise_adj(1, [(0, 4)])
        flip_adj(2, [0, 1])
        quantise_adj(1, [(4, 8)])
        flip_adj(2, [2, 3])
        g0 = acc_bank()
        multiply_tiles([0, 1, 2], g0, 0)
        quantise_adj(2, [(0, 4)])
        flip_adj(3, [0, 1])
        quantise_adj(2, [(4, 8)])
        flip_adj(3, [2, 3])
        multiply_tiles([3], g0, 0)
        g1 = acc_bank()
        multiply_tiles([4], g1, 4)
        quantise_adj(3, [(0, 4)])
        flip_adj(4, [0, 1])
        quantise_adj(3, [(4, 8)])
        flip_adj(4, [2, 3])
        multiply_tiles([5, 6], g1, 4)
        quantise_adj(4, [(0, 4)])
        finish([0, 1], g0, 's')
        flip_adj(5, [0, 1])
        quantise_adj(4, [(4, 8)])
        flip_adj(5, [2, 3])
        multiply_tiles([7], g1, 4)
        g2 = acc_bank()
        multiply_tiles([8], g2, 8)
        quantise_adj(5, [(0, 4)])
        flip_adj(6, [0, 1])
        quantise_adj(5, [(4, 8)])
        flip_adj(6, [2, 3])
        quantise_adj(6, [(0, 4)])
        finish([2, 3], g1, 's')
        flip_adj(7, [0, 1])
        quantise_adj(6, [(4, 8)])
        flip_adj(7, [2])
        quantise_adj(7, [(0, 4)])
        flip_last()
        quantise_adj(7, [(4, 6), (6, 7), (7, 8)])
        multiply_tiles([9, 10, 11], g2, 8)
        finish([4, 5], g2, 's')
        g3 = acc_bank()
        multiply_tiles([12, 13], g3, 12)
        finish([6], g3, 's')
        s14 = flip_bank()
        multiply_tile(7, 0, s14[:, :HID])
        finish_tile(7, 0, s14)
        s15 = flip_bank()
        multiply_tile(7, 1, s15[:, :HID])
        finish_tile(7, 1, s15)
